import numpy as np
import ml_dtypes


def mxq(x, axis, fmt="e4m3"):
    dtype, down = {"e4m3": (ml_dtypes.float8_e4m3fn, 7), "e5m2": (ml_dtypes.float8_e5m2, 14)}[fmt]
    v = np.moveaxis(np.asarray(x, np.float32).astype(ml_dtypes.bfloat16).astype(np.float64), axis, -1)
    blocks = v.reshape(v.shape[:-1] + (-1, 32))
    amax = np.abs(blocks).max(-1, keepdims=True)
    byte = np.maximum(np.where(amax > 0, np.frexp(amax)[1] - 1 + 127, 0) - down, 1)
    scale = np.exp2(byte - 127.0)
    codes = (blocks / scale).astype(np.float32).astype(dtype).astype(np.float64)
    return np.moveaxis((codes * scale).reshape(v.shape), -1, axis)


WIDE = False


def mx_kscale(k):
    if not WIDE:
        return np.ones(k)
    levels = np.array([10, -10, 5, -5, 0])
    a = np.random.permutation(np.resize(levels, k // 512 * 4)).reshape(k // 512, 4)
    idx = np.arange(k)
    return np.exp2(a[idx // 512, idx % 128 // 32])


BF16 = ml_dtypes.bfloat16


def bf(x):
    return np.asarray(x, np.float32).astype(BF16)


def f64(x):
    return np.asarray(x).astype(np.float64)


E2M1 = np.array([0.0, 0.5, 1.0, 1.5, 2.0, 3.0, 4.0, 6.0, -0.0, -0.5, -1.0, -1.5, -2.0, -3.0, -4.0, -6.0])


def pack_weight(w, fmt):
    k, n = w.shape
    w = f64(bf(w)).reshape(k // 32, 32, n)
    amax = np.abs(w).max(1)
    if fmt == "e4m3":
        byte = np.frexp(amax)[1] - 1 + 127 - 7
    else:
        mant, ex = np.frexp(amax / 6.0)
        byte = np.where(mant > 0.5, ex, ex - 1) + 127
    byte = np.clip(np.where(amax > 0, byte, 1), 1, 254)
    scaled = (w * np.exp2(127.0 - byte)[:, None, :]).reshape(k, n).astype(np.float32)
    by_word = np.ascontiguousarray(scaled.reshape(k // 512, 128, 4, n).transpose(0, 1, 3, 2))
    if fmt == "e4m3":
        words = by_word.astype(ml_dtypes.float8_e4m3fn).view(np.uint8)
    else:
        c = by_word.astype(ml_dtypes.float4_e2m1fn).view(np.uint8) & 0xF
        words = c[..., 0::2] | (c[..., 1::2] << 4)
    return np.ascontiguousarray(words), np.ascontiguousarray(byte.astype(np.uint8).reshape(k // 512, 16, n))


def unpack_weight(words, scales, fmt):
    g, p, n, _ = words.shape
    if fmt == "e4m3":
        vals = np.ascontiguousarray(words).view(ml_dtypes.float8_e4m3fn).astype(np.float64)
    else:
        nib = np.empty((g, p, n, 4), np.uint8)
        nib[..., 0::2] = words & 0xF
        nib[..., 1::2] = words >> 4
        vals = E2M1[nib]
    vals = vals * np.repeat(np.exp2(scales.astype(np.float64) - 127.0), 8, axis=1)[..., None]
    return vals.transpose(0, 1, 3, 2).reshape(g * 512, n)

def pack4(w):
    words, scales = pack_weight(w, "e2m1")
    return words.reshape(words.shape[0], 128, -1), scales


def unpack4(words, scales):
    return unpack_weight(words.reshape(words.shape[0], 128, -1, 2), scales, "e2m1")


B, T, C, D = 4, 512, 1024, 128
ROPE_BASE = 10000.0


def rotate_half(u):
    u1, u2 = np.split(u, 2, axis=-1)
    return np.concatenate([-u2, u1], axis=-1)


def rope_tables():
    inv_freq = 1.0 / (ROPE_BASE ** (f64(np.arange(0, D, 2)) / D))
    freqs = f64(np.arange(T))[:, None] * inv_freq[None, :]
    emb = np.concatenate([freqs, freqs], -1)
    return np.cos(emb), np.sin(emb)


def l2norm(u):
    return u / np.sqrt((u * u).sum(-1, keepdims=True))


def setup_inputs():
    s = mx_kscale(C)
    x = bf(np.random.standard_normal((B, T, C)) * s)
    w = np.random.standard_normal((3 * D, C)) / np.sqrt(C) / s
    words, scales = pack4(np.ascontiguousarray(w.T))
    sqk = bf(0.75 * (1.0 + 0.25 * np.random.standard_normal(D)))
    return {"x": x,
            "W_qkv_words": words,
            "W_qkv_scales": scales,
            "sqk": sqk}


def reference(x, W_qkv_words, W_qkv_scales, sqk):
    qkv = mxq(f64(x), 2, "e4m3") @ unpack4(W_qkv_words, W_qkv_scales)
    q, k, v = np.split(qkv, 3, axis=-1)
    cos, sin = rope_tables()
    q = q * cos + rotate_half(q) * sin
    k = k * cos + rotate_half(k) * sin
    g = f64(sqk)
    q = l2norm(q) * g
    k = l2norm(k) * g
    return q, k, v

@@ -1,0 +1,206 @@
+import math
+from contextlib import ExitStack
+
+import concourse.mybir as mybir
+from concourse.masks import make_identity
+
+F32 = mybir.dt.float32
+BF16 = mybir.dt.bfloat16
+I32 = mybir.dt.int32
+U32 = mybir.dt.uint32
+U8 = mybir.dt.uint8
+FP8X4 = mybir.dt.float8_e4m3fn_x4
+FP4X4 = mybir.dt.float4_e2m1fn_x4
+ALU = mybir.AluOpType
+ACT = mybir.ActivationFunctionType
+
+B, T, C, D = 4, 512, 1024, 128
+ROPE_BASE = 10000.0
+HALF = D // 2
+P = 128
+PACK = 4
+K_PASS = P * PACK
+PASSES = C // K_PASS
+WORDS_PER_PASS = K_PASS // 2
+TILES = T // P
+ROUND = 2
+ROUNDS_PER_BATCH = TILES // ROUND
+ROUNDS = B * ROUNDS_PER_BATCH
+QKV = 3
+ROUND_MAGIC = 1.5 * 2.0**23
+
+FLOPS = 2 * B * T * C * QKV * D
+
+
+def tile_attentionhead_pa_kernel(tc, x, W_qkv_words, W_qkv_scales, sqk, out_0, out_1, out_2):
+    nc = tc.nc
+    x_rows = x.rearrange("b (p a) k -> b p a k", a=TILES)
+    out_rows = [o.rearrange("b (p a) j -> b p a j", a=TILES) for o in (out_0, out_1, out_2)]
+
+    with ExitStack() as ctx:
+        consts = ctx.enter_context(tc.tile_pool(name="consts", bufs=1))
+        x_pool = ctx.enter_context(tc.tile_pool(name="x_pool", bufs=1))
+        stage = ctx.enter_context(tc.tile_pool(name="stage", bufs=3))
+        results = ctx.enter_context(tc.tile_pool(name="results", bufs=2))
+        psum_t = ctx.enter_context(tc.psum_pool(name="psum_t", bufs=4))
+        psum_o = ctx.enter_context(tc.psum_pool(name="psum_o", bufs=4))
+
+        x_tiles = [x_pool.tile([P, ROUND, C], BF16, name="x%d" % r) for r in range(ROUNDS)]
+
+        def load_x(r):
+            b, part = divmod(r, ROUNDS_PER_BATCH)
+            nc.sync.dma_start(out=x_tiles[r][:], in_=x_rows[b][:, part * ROUND : (part + 1) * ROUND, :])
+
+        load_x(0)
+
+        w_scales = consts.tile([P, PASSES, QKV * D], U8, align_bytes=64)
+        nc.vector.memset(w_scales[:].bitcast(I32), 0)
+        scale_rows = W_qkv_scales.rearrange("g (q r) n -> r q g n", r=4)
+        for r in range(4):
+            nc.sync.dma_start(out=w_scales[r:P:32].bitcast(I32), in_=scale_rows[r].bitcast(I32))
+        w_words = consts.tile([P, PASSES, 2 * QKV * D], U8, align_bytes=64)
+        nc.sync.dma_start(out=w_words[:].bitcast(I32), in_=W_qkv_words.rearrange("g p n -> p g n").bitcast(I32))
+
+        for r in range(1, ROUNDS):
+            load_x(r)
+
+        position_int = consts.tile([P, TILES], I32)
+        nc.gpsimd.iota(position_int[:], pattern=[[1, TILES]], base=0, channel_multiplier=TILES)
+        identity = consts.tile([P, P], F32)
+        make_identity(nc, identity[:])
+
+        gain_row = consts.tile([P, D], BF16)
+        nc.vector.memset(gain_row[:], 0.0)
+        nc.scalar.dma_start(out=gain_row[0:1, :], in_=sqk.unsqueeze(0))
+        ones = consts.tile([P, P], BF16)
+        nc.vector.memset(ones[:], 1.0)
+        gain = psum_t.tile([P, D], F32, tag="xt")
+        nc.tensor.matmul(out=gain[:], lhsT=ones[:], rhs=gain_row[:], start=True, stop=True)
+
+        frequency = consts.tile([P, HALF], F32)
+        nc.vector.memset(frequency[:, 0:1], 1.0)
+        for step in range(int(math.log2(HALF))):
+            w = 2**step
+            nc.vector.tensor_scalar_mul(
+                out=frequency[:, w : 2 * w], in0=frequency[:, 0:w], scalar1=ROPE_BASE ** (-2.0 * w / D)
+            )
+        position = consts.tile([P, TILES], F32)
+        nc.vector.tensor_copy(out=position[:], in_=position_int[:])
+        angle = consts.tile([P, TILES, HALF], F32)
+        nc.vector.tensor_tensor(
+            out=angle[:],
+            in0=position[:].unsqueeze(2).to_broadcast([P, TILES, HALF]),
+            in1=frequency[:].unsqueeze(1).to_broadcast([P, TILES, HALF]),
+            op=ALU.mult,
+        )
+        turns = consts.tile([P, 2, TILES, HALF], F32)
+        for i, shift in enumerate((0.25, 0.0)):
+            nc.vector.tensor_scalar(
+                out=turns[:, i], in0=angle[:], scalar1=1.0 / (2.0 * math.pi), scalar2=shift, op0=ALU.mult, op1=ALU.add
+            )
+        whole = consts.tile([P, 2, TILES, HALF], F32)
+        nc.vector.tensor_scalar_add(out=whole[:], in0=turns[:], scalar1=ROUND_MAGIC)
+        nc.vector.tensor_scalar_sub(out=whole[:], in0=whole[:], scalar1=ROUND_MAGIC)
+        part_turn = consts.tile([P, 2, TILES, HALF], F32)
+        nc.vector.tensor_sub(out=part_turn[:], in0=turns[:], in1=whole[:])
+        cos_sin = consts.tile([P, 2, TILES, HALF], F32)
+        nc.scalar.activation(out=cos_sin[:], in_=part_turn[:], func=ACT.Sin, scale=2.0 * math.pi)
+
+        tables = consts.tile([P, TILES, 2, D], F32)
+        table_halves = tables[:].rearrange("p a i (h c) -> p a i h c", h=2)
+        gain_halves = gain[:].rearrange("p (h c) -> p h c", h=2)
+        nc.vector.tensor_tensor(
+            out=table_halves[:, :, 0],
+            in0=cos_sin[:, 0].unsqueeze(2).to_broadcast([P, TILES, 2, HALF]),
+            in1=gain_halves.unsqueeze(1).to_broadcast([P, TILES, 2, HALF]),
+            op=ALU.mult,
+        )
+        nc.vector.tensor_tensor(
+            out=table_halves[:, :, 1, 0],
+            in0=cos_sin[:, 1],
+            in1=gain_halves[:, 1].unsqueeze(1).to_broadcast([P, TILES, HALF]),
+            op=ALU.mult,
+        )
+        nc.vector.scalar_tensor_tensor(
+            out=table_halves[:, :, 1, 1],
+            in0=cos_sin[:, 1],
+            scalar=-1.0,
+            in1=gain_halves[:, 0].unsqueeze(1).to_broadcast([P, TILES, HALF]),
+            op0=ALU.mult,
+            op1=ALU.mult,
+        )
+
+        def quantise_round(r):
+            grouped = stage.tile([P, ROUND * PASSES * P * PACK], BF16, align_bytes=64)
+            grouped_words = grouped[:].bitcast(F32).rearrange("p (i g t u) -> p i g t u", i=ROUND, g=PASSES, u=2)
+            for i in range(ROUND):
+                x_words = x_tiles[r][:, i, :].bitcast(F32)
+                xt = psum_t.tile([P, PASSES, 2, P], F32)
+                for g in range(PASSES):
+                    for u in range(2):
+                        first = g * WORDS_PER_PASS + u
+                        nc.tensor.transpose(xt[:, g, u, :], x_words[:, first : (g + 1) * WORDS_PER_PASS : 2], identity[:])
+                nc.scalar.copy(out=grouped_words[:, i], in_=xt[:].rearrange("p g u t -> p g t u"))
+            x_codes = stage.tile([P, ROUND, PASSES, P], U32, align_bytes=64)
+            x_scales = stage.tile([P, ROUND, PASSES, P], U8, align_bytes=64)
+            nc.vector.quantize_mx(
+                out=x_codes[:].rearrange("p i g t -> p (i g t)").bitcast(FP8X4),
+                scales=x_scales[:].rearrange("p i g t -> p (i g t)"),
+                in_=grouped[:],
+            )
+            return x_codes, x_scales
+
+        def project_round(r, x_codes, x_scales, result):
+            for i in range(ROUND):
+                a = (r % ROUNDS_PER_BATCH) * ROUND + i
+                qkv = psum_o.tile([P, QKV, D], F32)
+                for s in range(QKV):
+                    for g in range(PASSES):
+                        nc.tensor.matmul_mx(
+                            out=qkv[:, s, :],
+                            lhsT=x_codes[:, i, g, :].bitcast(FP8X4),
+                            lhsT_scale=x_scales[:, i, g, :],
+                            rhs=w_words[:, g, 2 * D * s : 2 * D * (s + 1)].bitcast(FP4X4),
+                            rhs_scale=w_scales[:, g, D * s : D * (s + 1)],
+                            start=(g == 0),
+                            stop=(g == PASSES - 1),
+                        )
+                squares = stage.tile([P, 2, D], BF16)
+                sum_squares = stage.tile([P, 2], F32)
+                for s in range(2):
+                    nc.scalar.activation(
+                        out=squares[:, s, :], in_=qkv[:, s, :], func=ACT.Square, accum_out=sum_squares[:, s : s + 1]
+                    )
+                nc.scalar.copy(out=result[:, 2, a, :], in_=qkv[:, 2, :])
+                inverse_norm = stage.tile([P, 2], F32)
+                nc.scalar.activation(out=inverse_norm[:], in_=sum_squares[:], func=ACT.Abs_reciprocal_sqrt)
+                products = stage.tile([P, 2, 2, D], F32)
+                for s in range(2):
+                    nc.vector.scalar_tensor_tensor(
+                        out=products[:, s],
+                        in0=qkv[:, s, :].unsqueeze(1).to_broadcast([P, 2, D]),
+                        scalar=inverse_norm[:, s : s + 1],
+                        in1=tables[:, a],
+                        op0=ALU.mult,
+                        op1=ALU.mult,
+                    )
+                for h in range(2):
+                    nc.vector.tensor_tensor(
+                        out=result[:, 0:2, a, h * HALF : (h + 1) * HALF],
+                        in0=products[:, :, 0, h * HALF : (h + 1) * HALF],
+                        in1=products[:, :, 1, (1 - h) * HALF : (2 - h) * HALF],
+                        op=ALU.add,
+                    )
+
+        quantised = {0: quantise_round(0)}
+        result = None
+        for r in range(ROUNDS):
+            if r + 1 < ROUNDS:
+                quantised[r + 1] = quantise_round(r + 1)
+            b, part = divmod(r, ROUNDS_PER_BATCH)
+            if part == 0:
+                result = results.tile([P, QKV, TILES, D], F32, name="result")
+            project_round(r, quantised[r][0], quantised[r][1], result)
+            if part == ROUNDS_PER_BATCH - 1:
+                for s in range(QKV):
+                    nc.sync.dma_start(out=out_rows[s][b], in_=result[:, s])

@@ -27,6 +27,7 @@ ROUND = 2
 ROUNDS_PER_BATCH = TILES // ROUND
 ROUNDS = B * ROUNDS_PER_BATCH
 QKV = 3
+VECTOR_COPIES_ONE_IN = 4
 ROUND_MAGIC = 1.5 * 2.0**23
 
 FLOPS = 2 * B * T * C * QKV * D
@@ -38,20 +39,21 @@ def tile_attentionhead_pa_kernel(tc, x, W_qkv_words, W_qkv_scales, sqk, out_0, o
     out_rows = [o.rearrange("b (p a) j -> b p a j", a=TILES) for o in (out_0, out_1, out_2)]
 
     with ExitStack() as ctx:
+        ctx.enter_context(tc.manual_schedule())
         consts = ctx.enter_context(tc.tile_pool(name="consts", bufs=1))
         x_pool = ctx.enter_context(tc.tile_pool(name="x_pool", bufs=1))
         stage = ctx.enter_context(tc.tile_pool(name="stage", bufs=3))
-        results = ctx.enter_context(tc.tile_pool(name="results", bufs=2))
-        psum_t = ctx.enter_context(tc.psum_pool(name="psum_t", bufs=4))
-        psum_o = ctx.enter_context(tc.psum_pool(name="psum_o", bufs=4))
+        results = ctx.enter_context(tc.tile_pool(name="results", bufs=ROUNDS))
+        psum_t = ctx.enter_context(tc.psum_pool(name="psum_t", bufs=2 * ROUND))
+        psum_o = ctx.enter_context(tc.psum_pool(name="psum_o", bufs=2 * ROUND))
 
-        x_tiles = [x_pool.tile([P, ROUND, C], BF16, name="x%d" % r) for r in range(ROUNDS)]
+        x_tiles = [x_pool.tile([P, C], BF16, name="x%d" % n) for n in range(B * TILES)]
 
-        def load_x(r):
-            b, part = divmod(r, ROUNDS_PER_BATCH)
-            nc.sync.dma_start(out=x_tiles[r][:], in_=x_rows[b][:, part * ROUND : (part + 1) * ROUND, :])
+        def load_x(n):
+            nc.sync.dma_start(out=x_tiles[n][:], in_=x_rows[n // TILES][:, n % TILES, :])
 
-        load_x(0)
+        for n in range(ROUND):
+            load_x(n)
 
         w_scales = consts.tile([P, PASSES, QKV * D], U8, align_bytes=64)
         nc.vector.memset(w_scales[:].bitcast(I32), 0)
@@ -61,8 +63,8 @@ def tile_attentionhead_pa_kernel(tc, x, W_qkv_words, W_qkv_scales, sqk, out_0, o
         w_words = consts.tile([P, PASSES, 2 * QKV * D], U8, align_bytes=64)
         nc.sync.dma_start(out=w_words[:].bitcast(I32), in_=W_qkv_words.rearrange("g p n -> p g n").bitcast(I32))
 
-        for r in range(1, ROUNDS):
-            load_x(r)
+        for n in range(ROUND, B * TILES):
+            load_x(n)
 
         position_int = consts.tile([P, TILES], I32)
         nc.gpsimd.iota(position_int[:], pattern=[[1, TILES]], base=0, channel_multiplier=TILES)
@@ -76,6 +78,10 @@ def tile_attentionhead_pa_kernel(tc, x, W_qkv_words, W_qkv_scales, sqk, out_0, o
         nc.vector.memset(ones[:], 1.0)
         gain = psum_t.tile([P, D], F32, tag="xt")
         nc.tensor.matmul(out=gain[:], lhsT=ones[:], rhs=gain_row[:], start=True, stop=True)
+        gains = consts.tile([P, 2, D], F32)
+        nc.scalar.copy(out=gains[:, 0, :], in_=gain[:])
+        nc.scalar.copy(out=gains[:, 1, 0:HALF], in_=gain[:, HALF:D])
+        nc.scalar.mul(out=gains[:, 1, HALF:D], in_=gain[:, 0:HALF], mul=-1.0)
 
         frequency = consts.tile([P, HALF], F32)
         nc.vector.memset(frequency[:, 0:1], 1.0)
@@ -105,55 +111,55 @@ def tile_attentionhead_pa_kernel(tc, x, W_qkv_words, W_qkv_scales, sqk, out_0, o
         nc.vector.tensor_sub(out=part_turn[:], in0=turns[:], in1=whole[:])
         cos_sin = consts.tile([P, 2, TILES, HALF], F32)
         nc.scalar.activation(out=cos_sin[:], in_=part_turn[:], func=ACT.Sin, scale=2.0 * math.pi)
+        table_load = consts.tile([P, 1], F32)
+        nc.scalar.activation(out=table_load[:], in_=frequency[:, 0:1], func=ACT.Abs_reciprocal_sqrt)
 
         tables = consts.tile([P, TILES, 2, D], F32)
-        table_halves = tables[:].rearrange("p a i (h c) -> p a i h c", h=2)
-        gain_halves = gain[:].rearrange("p (h c) -> p h c", h=2)
-        nc.vector.tensor_tensor(
-            out=table_halves[:, :, 0],
-            in0=cos_sin[:, 0].unsqueeze(2).to_broadcast([P, TILES, 2, HALF]),
-            in1=gain_halves.unsqueeze(1).to_broadcast([P, TILES, 2, HALF]),
-            op=ALU.mult,
-        )
-        nc.vector.tensor_tensor(
-            out=table_halves[:, :, 1, 0],
-            in0=cos_sin[:, 1],
-            in1=gain_halves[:, 1].unsqueeze(1).to_broadcast([P, TILES, HALF]),
-            op=ALU.mult,
-        )
-        nc.vector.scalar_tensor_tensor(
-            out=table_halves[:, :, 1, 1],
-            in0=cos_sin[:, 1],
-            scalar=-1.0,
-            in1=gain_halves[:, 0].unsqueeze(1).to_broadcast([P, TILES, HALF]),
-            op0=ALU.mult,
-            op1=ALU.mult,
-        )
+        for i in range(2):
+            nc.gpsimd.tensor_tensor(
+                out=tables[:, :, i, :].rearrange("p a (h c) -> p a h c", h=2),
+                in0=cos_sin[:, i].unsqueeze(2).to_broadcast([P, TILES, 2, HALF]),
+                in1=gains[:, i, :].rearrange("p (h c) -> p h c", h=2).unsqueeze(1).to_broadcast([P, TILES, 2, HALF]),
+                op=ALU.mult,
+            )
 
-        def quantise_round(r):
-            grouped = stage.tile([P, ROUND * PASSES * P * PACK], BF16, align_bytes=64)
-            grouped_words = grouped[:].bitcast(F32).rearrange("p (i g t u) -> p i g t u", i=ROUND, g=PASSES, u=2)
+        grouped = {}
+        quantised = {}
+        projected = {}
+
+        def transpose_round(r):
+            grouped[r] = stage.tile([P, ROUND * PASSES * P * PACK], BF16, align_bytes=64, name="grouped")
+            grouped_words = grouped[r][:].bitcast(F32).rearrange("p (i g t u) -> p i g t u", i=ROUND, g=PASSES, u=2)
             for i in range(ROUND):
-                x_words = x_tiles[r][:, i, :].bitcast(F32)
+                x_words = x_tiles[r * ROUND + i][:].bitcast(F32)
                 xt = psum_t.tile([P, PASSES, 2, P], F32)
                 for g in range(PASSES):
                     for u in range(2):
                         first = g * WORDS_PER_PASS + u
                         nc.tensor.transpose(xt[:, g, u, :], x_words[:, first : (g + 1) * WORDS_PER_PASS : 2], identity[:])
-                nc.scalar.copy(out=grouped_words[:, i], in_=xt[:].rearrange("p g u t -> p g t u"))
+                if (r * ROUND + i) % VECTOR_COPIES_ONE_IN == 0 or r == 0:
+                    nc.vector.tensor_copy(out=grouped_words[:, i], in_=xt[:].rearrange("p g u t -> p g t u"))
+                else:
+                    nc.scalar.copy(out=grouped_words[:, i], in_=xt[:].rearrange("p g u t -> p g t u"))
+
+        def quantise_round(r):
             x_codes = stage.tile([P, ROUND, PASSES, P], U32, align_bytes=64)
             x_scales = stage.tile([P, ROUND, PASSES, P], U8, align_bytes=64)
             nc.vector.quantize_mx(
                 out=x_codes[:].rearrange("p i g t -> p (i g t)").bitcast(FP8X4),
                 scales=x_scales[:].rearrange("p i g t -> p (i g t)"),
-                in_=grouped[:],
+                in_=grouped[r][:],
             )
-            return x_codes, x_scales
+            quantised[r] = (x_codes, x_scales)
 
-        def project_round(r, x_codes, x_scales, result):
+        def project_round(r):
+            x_codes, x_scales = quantised[r]
+            result = results.tile([P, QKV, ROUND, D], F32)
+            sum_squares = stage.tile([P, ROUND, 2], F32)
+            banks = []
             for i in range(ROUND):
-                a = (r % ROUNDS_PER_BATCH) * ROUND + i
                 qkv = psum_o.tile([P, QKV, D], F32)
+                banks.append(qkv)
                 for s in range(QKV):
                     for g in range(PASSES):
                         nc.tensor.matmul_mx(
@@ -165,42 +171,51 @@ def tile_attentionhead_pa_kernel(tc, x, W_qkv_words, W_qkv_scales, sqk, out_0, o
                             start=(g == 0),
                             stop=(g == PASSES - 1),
                         )
+            for i in range(ROUND):
                 squares = stage.tile([P, 2, D], BF16)
-                sum_squares = stage.tile([P, 2], F32)
                 for s in range(2):
                     nc.scalar.activation(
-                        out=squares[:, s, :], in_=qkv[:, s, :], func=ACT.Square, accum_out=sum_squares[:, s : s + 1]
+                        out=squares[:, s, :], in_=banks[i][:, s, :], func=ACT.Square, accum_out=sum_squares[:, i, s : s + 1]
                     )
-                nc.scalar.copy(out=result[:, 2, a, :], in_=qkv[:, 2, :])
-                inverse_norm = stage.tile([P, 2], F32)
-                nc.scalar.activation(out=inverse_norm[:], in_=sum_squares[:], func=ACT.Abs_reciprocal_sqrt)
-                products = stage.tile([P, 2, 2, D], F32)
+                nc.scalar.copy(out=result[:, 2, i, :], in_=banks[i][:, 2, :])
+            b, part = divmod(r, ROUNDS_PER_BATCH)
+            nc.sync.dma_start(out=out_rows[2][b][:, part * ROUND : (part + 1) * ROUND, :], in_=result[:, 2])
+            inverse_norm = stage.tile([P, ROUND, 2], F32)
+            nc.scalar.activation(out=inverse_norm[:], in_=sum_squares[:], func=ACT.Abs_reciprocal_sqrt)
+            projected[r] = (banks, inverse_norm, result)
+
+        def rotate_round(r):
+            banks, inverse_norm, result = projected[r]
+            b, part = divmod(r, ROUNDS_PER_BATCH)
+            products = stage.tile([P, ROUND, 2, 2, D], F32)
+            for i in range(ROUND):
                 for s in range(2):
                     nc.vector.scalar_tensor_tensor(
-                        out=products[:, s],
-                        in0=qkv[:, s, :].unsqueeze(1).to_broadcast([P, 2, D]),
-                        scalar=inverse_norm[:, s : s + 1],
-                        in1=tables[:, a],
+                        out=products[:, i, s],
+                        in0=banks[i][:, s, :].unsqueeze(1).to_broadcast([P, 2, D]),
+                        scalar=inverse_norm[:, i, s : s + 1],
+                        in1=tables[:, part * ROUND + i],
                         op0=ALU.mult,
                         op1=ALU.mult,
                     )
-                for h in range(2):
-                    nc.vector.tensor_tensor(
-                        out=result[:, 0:2, a, h * HALF : (h + 1) * HALF],
-                        in0=products[:, :, 0, h * HALF : (h + 1) * HALF],
-                        in1=products[:, :, 1, (1 - h) * HALF : (2 - h) * HALF],
-                        op=ALU.add,
-                    )
+            rotated = result[:, 0:2].rearrange("p s i j -> p i s j")
+            adder = nc.vector if r == ROUNDS - 1 else nc.gpsimd
+            for h in range(2):
+                adder.tensor_tensor(
+                    out=rotated[:, :, :, h * HALF : (h + 1) * HALF],
+                    in0=products[:, :, :, 0, h * HALF : (h + 1) * HALF],
+                    in1=products[:, :, :, 1, (1 - h) * HALF : (2 - h) * HALF],
+                    op=ALU.add,
+                )
+            for s in range(2):
+                nc.sync.dma_start(out=out_rows[s][b][:, part * ROUND : (part + 1) * ROUND, :], in_=result[:, s])
 
-        quantised = {0: quantise_round(0)}
-        result = None
-        for r in range(ROUNDS):
-            if r + 1 < ROUNDS:
-                quantised[r + 1] = quantise_round(r + 1)
-            b, part = divmod(r, ROUNDS_PER_BATCH)
-            if part == 0:
-                result = results.tile([P, QKV, TILES, D], F32, name="result")
-            project_round(r, quantised[r][0], quantised[r][1], result)
-            if part == ROUNDS_PER_BATCH - 1:
-                for s in range(QKV):
-                    nc.sync.dma_start(out=out_rows[s][b], in_=result[:, s])
+        for step in range(ROUNDS + 2):
+            if step < ROUNDS:
+                transpose_round(step)
+            if step >= 2:
+                rotate_round(step - 2)
+            if step < ROUNDS:
+                quantise_round(step)
+            if 1 <= step <= ROUNDS:
+                project_round(step - 1)

@@ -45,7 +45,7 @@ def tile_attentionhead_pa_kernel(tc, x, W_qkv_words, W_qkv_scales, sqk, out_0, o
         stage = ctx.enter_context(tc.tile_pool(name="stage", bufs=3))
         results = ctx.enter_context(tc.tile_pool(name="results", bufs=ROUNDS))
         psum_t = ctx.enter_context(tc.psum_pool(name="psum_t", bufs=2 * ROUND))
-        psum_o = ctx.enter_context(tc.psum_pool(name="psum_o", bufs=2 * ROUND))
+        psum_o = ctx.enter_context(tc.psum_pool(name="psum_o", bufs=2))
 
         x_tiles = [x_pool.tile([P, C], BF16, name="x%d" % n) for n in range(B * TILES)]
 
@@ -66,8 +66,10 @@ def tile_attentionhead_pa_kernel(tc, x, W_qkv_words, W_qkv_scales, sqk, out_0, o
         for n in range(ROUND, B * TILES):
             load_x(n)
 
-        position_int = consts.tile([P, TILES], I32)
-        nc.gpsimd.iota(position_int[:], pattern=[[1, TILES]], base=0, channel_multiplier=TILES)
+        position = consts.tile([P, TILES], F32)
+        nc.gpsimd.iota(
+            position[:], pattern=[[1, TILES]], base=0, channel_multiplier=TILES, allow_small_or_imprecise_dtypes=True
+        )
         identity = consts.tile([P, P], F32)
         make_identity(nc, identity[:])
 
@@ -78,10 +80,6 @@ def tile_attentionhead_pa_kernel(tc, x, W_qkv_words, W_qkv_scales, sqk, out_0, o
         nc.vector.memset(ones[:], 1.0)
         gain = psum_t.tile([P, D], F32, tag="xt")
         nc.tensor.matmul(out=gain[:], lhsT=ones[:], rhs=gain_row[:], start=True, stop=True)
-        gains = consts.tile([P, 2, D], F32)
-        nc.scalar.copy(out=gains[:, 0, :], in_=gain[:])
-        nc.scalar.copy(out=gains[:, 1, 0:HALF], in_=gain[:, HALF:D])
-        nc.scalar.mul(out=gains[:, 1, HALF:D], in_=gain[:, 0:HALF], mul=-1.0)
 
         frequency = consts.tile([P, HALF], F32)
         nc.vector.memset(frequency[:, 0:1], 1.0)
@@ -90,38 +88,43 @@ def tile_attentionhead_pa_kernel(tc, x, W_qkv_words, W_qkv_scales, sqk, out_0, o
             nc.vector.tensor_scalar_mul(
                 out=frequency[:, w : 2 * w], in0=frequency[:, 0:w], scalar1=ROPE_BASE ** (-2.0 * w / D)
             )
-        position = consts.tile([P, TILES], F32)
-        nc.vector.tensor_copy(out=position[:], in_=position_int[:])
-        angle = consts.tile([P, TILES, HALF], F32)
+        position_turns = consts.tile([P, TILES], F32)
+        nc.vector.tensor_scalar_mul(out=position_turns[:], in0=position[:], scalar1=1.0 / (2.0 * math.pi))
+        turns = consts.tile([P, TILES, HALF], F32)
         nc.vector.tensor_tensor(
-            out=angle[:],
-            in0=position[:].unsqueeze(2).to_broadcast([P, TILES, HALF]),
+            out=turns[:],
+            in0=position_turns[:].unsqueeze(2).to_broadcast([P, TILES, HALF]),
             in1=frequency[:].unsqueeze(1).to_broadcast([P, TILES, HALF]),
             op=ALU.mult,
         )
-        turns = consts.tile([P, 2, TILES, HALF], F32)
-        for i, shift in enumerate((0.25, 0.0)):
-            nc.vector.tensor_scalar(
-                out=turns[:, i], in0=angle[:], scalar1=1.0 / (2.0 * math.pi), scalar2=shift, op0=ALU.mult, op1=ALU.add
-            )
-        whole = consts.tile([P, 2, TILES, HALF], F32)
-        nc.vector.tensor_scalar_add(out=whole[:], in0=turns[:], scalar1=ROUND_MAGIC)
-        nc.vector.tensor_scalar_sub(out=whole[:], in0=whole[:], scalar1=ROUND_MAGIC)
-        part_turn = consts.tile([P, 2, TILES, HALF], F32)
+        whole = consts.tile([P, TILES, HALF], F32)
+        nc.vector.tensor_scalar(
+            out=whole[:], in0=turns[:], scalar1=ROUND_MAGIC, scalar2=ROUND_MAGIC, op0=ALU.add, op1=ALU.subtract
+        )
+        part_turn = consts.tile([P, TILES, HALF], F32)
         nc.vector.tensor_sub(out=part_turn[:], in0=turns[:], in1=whole[:])
+        gains = consts.tile([P, 2, D], F32)
+        nc.vector.tensor_copy(out=gains[:, 0, :], in_=gain[:])
+        nc.vector.tensor_copy(out=gains[:, 1, 0:HALF], in_=gain[:, HALF:D])
+        nc.vector.tensor_scalar_mul(out=gains[:, 1, HALF:D], in0=gain[:, 0:HALF], scalar1=-1.0)
+        part_turn_abs = consts.tile([P, TILES, HALF], F32)
+        nc.scalar.activation(out=part_turn_abs[:], in_=part_turn[:], func=ACT.Abs)
         cos_sin = consts.tile([P, 2, TILES, HALF], F32)
-        nc.scalar.activation(out=cos_sin[:], in_=part_turn[:], func=ACT.Sin, scale=2.0 * math.pi)
+        nc.scalar.activation(out=cos_sin[:, 1], in_=part_turn[:], func=ACT.Sin, scale=2.0 * math.pi)
+        nc.scalar.activation(out=cos_sin[:, 0], in_=part_turn_abs[:], func=ACT.Sin, scale=-2.0 * math.pi, bias=math.pi / 2.0)
         table_load = consts.tile([P, 1], F32)
         nc.scalar.activation(out=table_load[:], in_=frequency[:, 0:1], func=ACT.Abs_reciprocal_sqrt)
 
         tables = consts.tile([P, TILES, 2, D], F32)
-        for i in range(2):
-            nc.gpsimd.tensor_tensor(
-                out=tables[:, :, i, :].rearrange("p a (h c) -> p a h c", h=2),
-                in0=cos_sin[:, i].unsqueeze(2).to_broadcast([P, TILES, 2, HALF]),
-                in1=gains[:, i, :].rearrange("p (h c) -> p h c", h=2).unsqueeze(1).to_broadcast([P, TILES, 2, HALF]),
-                op=ALU.mult,
-            )
+        for part in range(ROUNDS_PER_BATCH):
+            tiles = slice(part * ROUND, (part + 1) * ROUND)
+            for i in range(2):
+                nc.gpsimd.tensor_tensor(
+                    out=tables[:, tiles, i, :].rearrange("p a (h c) -> p a h c", h=2),
+                    in0=cos_sin[:, i, tiles].unsqueeze(2).to_broadcast([P, ROUND, 2, HALF]),
+                    in1=gains[:, i, :].rearrange("p (h c) -> p h c", h=2).unsqueeze(1).to_broadcast([P, ROUND, 2, HALF]),
+                    op=ALU.mult,
+                )
 
         grouped = {}
         quantised = {}
@@ -154,45 +157,51 @@ def tile_attentionhead_pa_kernel(tc, x, W_qkv_words, W_qkv_scales, sqk, out_0, o
 
         def project_round(r):
             x_codes, x_scales = quantised[r]
-            result = results.tile([P, QKV, ROUND, D], F32)
+            b, part = divmod(r, ROUNDS_PER_BATCH)
+
+            def project(out, i, s):
+                for g in range(PASSES):
+                    nc.tensor.matmul_mx(
+                        out=out,
+                        lhsT=x_codes[:, i, g, :].bitcast(FP8X4),
+                        lhsT_scale=x_scales[:, i, g, :],
+                        rhs=w_words[:, g, 2 * D * s : 2 * D * (s + 1)].bitcast(FP4X4),
+                        rhs_scale=w_scales[:, g, D * s : D * (s + 1)],
+                        start=(g == 0),
+                        stop=(g == PASSES - 1),
+                    )
+
+            qk = psum_o.tile([P, ROUND, 2, D], F32)
+            for i in range(ROUND):
+                for s in range(2):
+                    project(qk[:, i, s, :], i, s)
+            v = psum_o.tile([P, ROUND, D], F32)
+            for i in range(ROUND):
+                project(v[:, i, :], i, 2)
+
+            squares = stage.tile([P, ROUND, 2, D], BF16)
             sum_squares = stage.tile([P, ROUND, 2], F32)
-            banks = []
             for i in range(ROUND):
-                qkv = psum_o.tile([P, QKV, D], F32)
-                banks.append(qkv)
-                for s in range(QKV):
-                    for g in range(PASSES):
-                        nc.tensor.matmul_mx(
-                            out=qkv[:, s, :],
-                            lhsT=x_codes[:, i, g, :].bitcast(FP8X4),
-                            lhsT_scale=x_scales[:, i, g, :],
-                            rhs=w_words[:, g, 2 * D * s : 2 * D * (s + 1)].bitcast(FP4X4),
-                            rhs_scale=w_scales[:, g, D * s : D * (s + 1)],
-                            start=(g == 0),
-                            stop=(g == PASSES - 1),
-                        )
-            for i in range(ROUND):
-                squares = stage.tile([P, 2, D], BF16)
                 for s in range(2):
                     nc.scalar.activation(
-                        out=squares[:, s, :], in_=banks[i][:, s, :], func=ACT.Square, accum_out=sum_squares[:, i, s : s + 1]
+                        out=squares[:, i, s, :], in_=qk[:, i, s, :], func=ACT.Square, accum_out=sum_squares[:, i, s : s + 1]
                     )
-                nc.scalar.copy(out=result[:, 2, i, :], in_=banks[i][:, 2, :])
-            b, part = divmod(r, ROUNDS_PER_BATCH)
-            nc.sync.dma_start(out=out_rows[2][b][:, part * ROUND : (part + 1) * ROUND, :], in_=result[:, 2])
             inverse_norm = stage.tile([P, ROUND, 2], F32)
             nc.scalar.activation(out=inverse_norm[:], in_=sum_squares[:], func=ACT.Abs_reciprocal_sqrt)
-            projected[r] = (banks, inverse_norm, result)
+            result = results.tile([P, QKV, ROUND, D], F32)
+            nc.scalar.copy(out=result[:, 2], in_=v[:])
+            nc.sync.dma_start(out=out_rows[2][b][:, part * ROUND : (part + 1) * ROUND, :], in_=result[:, 2])
+            projected[r] = (qk, inverse_norm, result)
 
         def rotate_round(r):
-            banks, inverse_norm, result = projected[r]
+            qk, inverse_norm, result = projected[r]
             b, part = divmod(r, ROUNDS_PER_BATCH)
             products = stage.tile([P, ROUND, 2, 2, D], F32)
             for i in range(ROUND):
                 for s in range(2):
                     nc.vector.scalar_tensor_tensor(
                         out=products[:, i, s],
-                        in0=banks[i][:, s, :].unsqueeze(1).to_broadcast([P, 2, D]),
+                        in0=qk[:, i, s, :].unsqueeze(1).to_broadcast([P, 2, D]),
                         scalar=inverse_norm[:, i, s : s + 1],
                         in1=tables[:, part * ROUND + i],
                         op0=ALU.mult,

@@ -45,14 +45,14 @@ def tile_attentionhead_pa_kernel(tc, x, W_qkv_words, W_qkv_scales, sqk, out_0, o
         stage = ctx.enter_context(tc.tile_pool(name="stage", bufs=3))
         results = ctx.enter_context(tc.tile_pool(name="results", bufs=ROUNDS))
         psum_t = ctx.enter_context(tc.psum_pool(name="psum_t", bufs=2 * ROUND))
-        psum_o = ctx.enter_context(tc.psum_pool(name="psum_o", bufs=2))
+        psum_o = ctx.enter_context(tc.psum_pool(name="psum_o", bufs=2 * ROUND))
 
         x_tiles = [x_pool.tile([P, C], BF16, name="x%d" % n) for n in range(B * TILES)]
 
         def load_x(n):
             nc.sync.dma_start(out=x_tiles[n][:], in_=x_rows[n // TILES][:, n % TILES, :])
 
-        for n in range(ROUND):
+        for n in range(2 * ROUND):
             load_x(n)
 
         w_scales = consts.tile([P, PASSES, QKV * D], U8, align_bytes=64)
@@ -63,7 +63,7 @@ def tile_attentionhead_pa_kernel(tc, x, W_qkv_words, W_qkv_scales, sqk, out_0, o
         w_words = consts.tile([P, PASSES, 2 * QKV * D], U8, align_bytes=64)
         nc.sync.dma_start(out=w_words[:].bitcast(I32), in_=W_qkv_words.rearrange("g p n -> p g n").bitcast(I32))
 
-        for n in range(ROUND, B * TILES):
+        for n in range(2 * ROUND, B * TILES):
             load_x(n)
 
         position = consts.tile([P, TILES], F32)
@@ -148,60 +148,56 @@ def tile_attentionhead_pa_kernel(tc, x, W_qkv_words, W_qkv_scales, sqk, out_0, o
         def quantise_round(r):
             x_codes = stage.tile([P, ROUND, PASSES, P], U32, align_bytes=64)
             x_scales = stage.tile([P, ROUND, PASSES, P], U8, align_bytes=64)
-            nc.vector.quantize_mx(
-                out=x_codes[:].rearrange("p i g t -> p (i g t)").bitcast(FP8X4),
-                scales=x_scales[:].rearrange("p i g t -> p (i g t)"),
-                in_=grouped[r][:],
-            )
+            tile_values = PASSES * P * PACK
+            for i in range(ROUND):
+                nc.vector.quantize_mx(
+                    out=x_codes[:, i].rearrange("p g t -> p (g t)").bitcast(FP8X4),
+                    scales=x_scales[:, i].rearrange("p g t -> p (g t)"),
+                    in_=grouped[r][:, i * tile_values : (i + 1) * tile_values],
+                )
             quantised[r] = (x_codes, x_scales)
 
         def project_round(r):
             x_codes, x_scales = quantised[r]
-            b, part = divmod(r, ROUNDS_PER_BATCH)
-
-            def project(out, i, s):
-                for g in range(PASSES):
-                    nc.tensor.matmul_mx(
-                        out=out,
-                        lhsT=x_codes[:, i, g, :].bitcast(FP8X4),
-                        lhsT_scale=x_scales[:, i, g, :],
-                        rhs=w_words[:, g, 2 * D * s : 2 * D * (s + 1)].bitcast(FP4X4),
-                        rhs_scale=w_scales[:, g, D * s : D * (s + 1)],
-                        start=(g == 0),
-                        stop=(g == PASSES - 1),
-                    )
-
-            qk = psum_o.tile([P, ROUND, 2, D], F32)
-            for i in range(ROUND):
-                for s in range(2):
-                    project(qk[:, i, s, :], i, s)
-            v = psum_o.tile([P, ROUND, D], F32)
-            for i in range(ROUND):
-                project(v[:, i, :], i, 2)
-
-            squares = stage.tile([P, ROUND, 2, D], BF16)
+            result = results.tile([P, QKV, ROUND, D], F32)
             sum_squares = stage.tile([P, ROUND, 2], F32)
+            inverse_norm = stage.tile([P, ROUND, 2], F32)
+            banks = []
             for i in range(ROUND):
+                qkv = psum_o.tile([P, QKV, D], F32)
+                banks.append(qkv)
+                for s in range(QKV):
+                    for g in range(PASSES):
+                        nc.tensor.matmul_mx(
+                            out=qkv[:, s, :],
+                            lhsT=x_codes[:, i, g, :].bitcast(FP8X4),
+                            lhsT_scale=x_scales[:, i, g, :],
+                            rhs=w_words[:, g, 2 * D * s : 2 * D * (s + 1)].bitcast(FP4X4),
+                            rhs_scale=w_scales[:, g, D * s : D * (s + 1)],
+                            start=(g == 0),
+                            stop=(g == PASSES - 1),
+                        )
+            for i in range(ROUND):
+                squares = stage.tile([P, 2, D], BF16)
                 for s in range(2):
                     nc.scalar.activation(
-                        out=squares[:, i, s, :], in_=qk[:, i, s, :], func=ACT.Square, accum_out=sum_squares[:, i, s : s + 1]
+                        out=squares[:, s, :], in_=banks[i][:, s, :], func=ACT.Square, accum_out=sum_squares[:, i, s : s + 1]
                     )
-            inverse_norm = stage.tile([P, ROUND, 2], F32)
-            nc.scalar.activation(out=inverse_norm[:], in_=sum_squares[:], func=ACT.Abs_reciprocal_sqrt)
-            result = results.tile([P, QKV, ROUND, D], F32)
-            nc.scalar.copy(out=result[:, 2], in_=v[:])
+                nc.scalar.copy(out=result[:, 2, i, :], in_=banks[i][:, 2, :])
+                nc.scalar.activation(out=inverse_norm[:, i], in_=sum_squares[:, i], func=ACT.Abs_reciprocal_sqrt)
+            b, part = divmod(r, ROUNDS_PER_BATCH)
             nc.sync.dma_start(out=out_rows[2][b][:, part * ROUND : (part + 1) * ROUND, :], in_=result[:, 2])
-            projected[r] = (qk, inverse_norm, result)
+            projected[r] = (banks, inverse_norm, result)
 
         def rotate_round(r):
-            qk, inverse_norm, result = projected[r]
+            banks, inverse_norm, result = projected[r]
             b, part = divmod(r, ROUNDS_PER_BATCH)
             products = stage.tile([P, ROUND, 2, 2, D], F32)
             for i in range(ROUND):
                 for s in range(2):
                     nc.vector.scalar_tensor_tensor(
                         out=products[:, i, s],
-                        in0=qk[:, i, s, :].unsqueeze(1).to_broadcast([P, 2, D]),
+                        in0=banks[i][:, s, :].unsqueeze(1).to_broadcast([P, 2, D]),
                         scalar=inverse_norm[:, i, s : s + 1],
                         in1=tables[:, part * ROUND + i],
                         op0=ALU.mult,

@@ -78,8 +78,6 @@ def tile_attentionhead_pa_kernel(tc, x, W_qkv_words, W_qkv_scales, sqk, out_0, o
         nc.scalar.dma_start(out=gain_row[0:1, :], in_=sqk.unsqueeze(0))
         ones = consts.tile([P, P], BF16)
         nc.vector.memset(ones[:], 1.0)
-        gain = psum_t.tile([P, D], F32, tag="xt")
-        nc.tensor.matmul(out=gain[:], lhsT=ones[:], rhs=gain_row[:], start=True, stop=True)
 
         frequency = consts.tile([P, HALF], F32)
         nc.vector.memset(frequency[:, 0:1], 1.0)
@@ -103,12 +101,10 @@ def tile_attentionhead_pa_kernel(tc, x, W_qkv_words, W_qkv_scales, sqk, out_0, o
         )
         part_turn = consts.tile([P, TILES, HALF], F32)
         nc.vector.tensor_sub(out=part_turn[:], in0=turns[:], in1=whole[:])
-        gains = consts.tile([P, 2, D], F32)
-        nc.vector.tensor_copy(out=gains[:, 0, :], in_=gain[:])
-        nc.vector.tensor_copy(out=gains[:, 1, 0:HALF], in_=gain[:, HALF:D])
-        nc.vector.tensor_scalar_mul(out=gains[:, 1, HALF:D], in0=gain[:, 0:HALF], scalar1=-1.0)
         part_turn_abs = consts.tile([P, TILES, HALF], F32)
-        nc.scalar.activation(out=part_turn_abs[:], in_=part_turn[:], func=ACT.Abs)
+        nc.vector.scalar_tensor_tensor(
+            out=part_turn_abs[:], in0=part_turn[:], scalar=-1.0, in1=part_turn[:], op0=ALU.mult, op1=ALU.max
+        )
         cos_sin = consts.tile([P, 2, TILES, HALF], F32)
         nc.scalar.activation(out=cos_sin[:, 1], in_=part_turn[:], func=ACT.Sin, scale=2.0 * math.pi)
         nc.scalar.activation(out=cos_sin[:, 0], in_=part_turn_abs[:], func=ACT.Sin, scale=-2.0 * math.pi, bias=math.pi / 2.0)
@@ -116,15 +112,23 @@ def tile_attentionhead_pa_kernel(tc, x, W_qkv_words, W_qkv_scales, sqk, out_0, o
         nc.scalar.activation(out=table_load[:], in_=frequency[:, 0:1], func=ACT.Abs_reciprocal_sqrt)
 
         tables = consts.tile([P, TILES, 2, D], F32)
-        for part in range(ROUNDS_PER_BATCH):
-            tiles = slice(part * ROUND, (part + 1) * ROUND)
-            for i in range(2):
-                nc.gpsimd.tensor_tensor(
-                    out=tables[:, tiles, i, :].rearrange("p a (h c) -> p a h c", h=2),
-                    in0=cos_sin[:, i, tiles].unsqueeze(2).to_broadcast([P, ROUND, 2, HALF]),
-                    in1=gains[:, i, :].rearrange("p (h c) -> p h c", h=2).unsqueeze(1).to_broadcast([P, ROUND, 2, HALF]),
-                    op=ALU.mult,
-                )
+
+        def build_tables():
+            gain = psum_t.tile([P, D], F32, tag="xt")
+            nc.tensor.matmul(out=gain[:], lhsT=ones[:], rhs=gain_row[:], start=True, stop=True)
+            gains = consts.tile([P, 2, D], F32)
+            nc.scalar.copy(out=gains[:, 0, :], in_=gain[:])
+            nc.scalar.copy(out=gains[:, 1, 0:HALF], in_=gain[:, HALF:D])
+            nc.scalar.mul(out=gains[:, 1, HALF:D], in_=gain[:, 0:HALF], mul=-1.0)
+            for part in range(ROUNDS_PER_BATCH):
+                tiles = slice(part * ROUND, (part + 1) * ROUND)
+                for i in range(2):
+                    nc.gpsimd.tensor_tensor(
+                        out=tables[:, tiles, i, :].rearrange("p a (h c) -> p a h c", h=2),
+                        in0=cos_sin[:, i, tiles].unsqueeze(2).to_broadcast([P, ROUND, 2, HALF]),
+                        in1=gains[:, i, :].rearrange("p (h c) -> p h c", h=2).unsqueeze(1).to_broadcast([P, ROUND, 2, HALF]),
+                        op=ALU.mult,
+                    )
 
         grouped = {}
         quantised = {}
@@ -140,7 +144,7 @@ def tile_attentionhead_pa_kernel(tc, x, W_qkv_words, W_qkv_scales, sqk, out_0, o
                     for u in range(2):
                         first = g * WORDS_PER_PASS + u
                         nc.tensor.transpose(xt[:, g, u, :], x_words[:, first : (g + 1) * WORDS_PER_PASS : 2], identity[:])
-                if (r * ROUND + i) % VECTOR_COPIES_ONE_IN == 0 or r == 0:
+                if r < 2 or (r * ROUND + i) % VECTOR_COPIES_ONE_IN == 0:
                     nc.vector.tensor_copy(out=grouped_words[:, i], in_=xt[:].rearrange("p g u t -> p g t u"))
                 else:
                     nc.scalar.copy(out=grouped_words[:, i], in_=xt[:].rearrange("p g u t -> p g t u"))
@@ -218,6 +222,8 @@ def tile_attentionhead_pa_kernel(tc, x, W_qkv_words, W_qkv_scales, sqk, out_0, o
         for step in range(ROUNDS + 2):
             if step < ROUNDS:
                 transpose_round(step)
+            if step == 0:
+                build_tables()
             if step >= 2:
                 rotate_round(step - 2)
             if step < ROUNDS:

@@ -208,14 +208,23 @@ def tile_attentionhead_pa_kernel(tc, x, W_qkv_words, W_qkv_scales, sqk, out_0, o
                         op1=ALU.mult,
                     )
             rotated = result[:, 0:2].rearrange("p s i j -> p i s j")
-            adder = nc.vector if r == ROUNDS - 1 else nc.gpsimd
-            for h in range(2):
-                adder.tensor_tensor(
-                    out=rotated[:, :, :, h * HALF : (h + 1) * HALF],
-                    in0=products[:, :, :, 0, h * HALF : (h + 1) * HALF],
-                    in1=products[:, :, :, 1, (1 - h) * HALF : (2 - h) * HALF],
-                    op=ALU.add,
-                )
+            if r < ROUNDS - 2:
+                for h in range(2):
+                    nc.gpsimd.tensor_tensor(
+                        out=rotated[:, :, :, h * HALF : (h + 1) * HALF],
+                        in0=products[:, :, :, 0, h * HALF : (h + 1) * HALF],
+                        in1=products[:, :, :, 1, (1 - h) * HALF : (2 - h) * HALF],
+                        op=ALU.add,
+                    )
+            else:
+                adder = nc.vector if r == ROUNDS - 1 else nc.gpsimd
+                for i in range(ROUND):
+                    adder.tensor_tensor(
+                        out=rotated[:, i].rearrange("p s (h c) -> p s h c", h=2),
+                        in0=products[:, i, :, 0, :].rearrange("p s (h c) -> p s h c", h=2),
+                        in1=products[:, i, :, 1, :].rearrange("p s (h c) -> p s h c", h=2)[:, :, ::-1, :],
+                        op=ALU.add,
+                    )
             for s in range(2):
                 nc.sync.dma_start(out=out_rows[s][b][:, part * ROUND : (part + 1) * ROUND, :], in_=result[:, s])
 

@@ -27,7 +27,6 @@ ROUND = 2
 ROUNDS_PER_BATCH = TILES // ROUND
 ROUNDS = B * ROUNDS_PER_BATCH
 QKV = 3
-VECTOR_COPIES_ONE_IN = 4
 ROUND_MAGIC = 1.5 * 2.0**23
 
 FLOPS = 2 * B * T * C * QKV * D
@@ -144,8 +143,11 @@ def tile_attentionhead_pa_kernel(tc, x, W_qkv_words, W_qkv_scales, sqk, out_0, o
                     for u in range(2):
                         first = g * WORDS_PER_PASS + u
                         nc.tensor.transpose(xt[:, g, u, :], x_words[:, first : (g + 1) * WORDS_PER_PASS : 2], identity[:])
-                if r < 2 or (r * ROUND + i) % VECTOR_COPIES_ONE_IN == 0:
+                if r < 2:
                     nc.vector.tensor_copy(out=grouped_words[:, i], in_=xt[:].rearrange("p g u t -> p g t u"))
+                elif i == 0:
+                    nc.vector.tensor_copy(out=grouped_words[:, i, 0], in_=xt[:, 0].rearrange("p u t -> p t u"))
+                    nc.scalar.copy(out=grouped_words[:, i, 1], in_=xt[:, 1].rearrange("p u t -> p t u"))
                 else:
                     nc.scalar.copy(out=grouped_words[:, i], in_=xt[:].rearrange("p g u t -> p g t u"))
 

@@ -198,33 +198,31 @@ def tile_attentionhead_pa_kernel(tc, x, W_qkv_words, W_qkv_scales, sqk, out_0, o
         def rotate_round(r):
             banks, inverse_norm, result = projected[r]
             b, part = divmod(r, ROUNDS_PER_BATCH)
-            products = stage.tile([P, ROUND, 2, 2, D], F32)
+            products = stage.tile([P, 2, ROUND, 2, D], F32)
             for i in range(ROUND):
                 for s in range(2):
                     nc.vector.scalar_tensor_tensor(
-                        out=products[:, i, s],
+                        out=products[:, s, i],
                         in0=banks[i][:, s, :].unsqueeze(1).to_broadcast([P, 2, D]),
                         scalar=inverse_norm[:, i, s : s + 1],
                         in1=tables[:, part * ROUND + i],
                         op0=ALU.mult,
                         op1=ALU.mult,
                     )
-            rotated = result[:, 0:2].rearrange("p s i j -> p i s j")
             if r < ROUNDS - 2:
-                for h in range(2):
-                    nc.gpsimd.tensor_tensor(
-                        out=rotated[:, :, :, h * HALF : (h + 1) * HALF],
-                        in0=products[:, :, :, 0, h * HALF : (h + 1) * HALF],
-                        in1=products[:, :, :, 1, (1 - h) * HALF : (2 - h) * HALF],
-                        op=ALU.add,
-                    )
+                nc.gpsimd.tensor_tensor(
+                    out=result[:, 0:2].rearrange("p s i (h c) -> p (s i) h c", h=2),
+                    in0=products[:, :, :, 0, :].rearrange("p s i (h c) -> p (s i) h c", h=2),
+                    in1=products[:, :, :, 1, :].rearrange("p s i (h c) -> p (s i) h c", h=2)[:, :, ::-1, :],
+                    op=ALU.add,
+                )
             else:
                 adder = nc.vector if r == ROUNDS - 1 else nc.gpsimd
                 for i in range(ROUND):
                     adder.tensor_tensor(
-                        out=rotated[:, i].rearrange("p s (h c) -> p s h c", h=2),
-                        in0=products[:, i, :, 0, :].rearrange("p s (h c) -> p s h c", h=2),
-                        in1=products[:, i, :, 1, :].rearrange("p s (h c) -> p s h c", h=2)[:, :, ::-1, :],
+                        out=result[:, 0:2, i, :].rearrange("p s (h c) -> p s h c", h=2),
+                        in0=products[:, :, i, 0, :].rearrange("p s (h c) -> p s h c", h=2),
+                        in1=products[:, :, i, 1, :].rearrange("p s (h c) -> p s h c", h=2)[:, :, ::-1, :],
                         op=ALU.add,
                     )
             for s in range(2):

@@ -209,17 +209,17 @@ def tile_attentionhead_pa_kernel(tc, x, W_qkv_words, W_qkv_scales, sqk, out_0, o
                         op0=ALU.mult,
                         op1=ALU.mult,
                     )
-            if r < ROUNDS - 2:
-                nc.gpsimd.tensor_tensor(
+            if r != ROUNDS - 2:
+                adder = nc.vector if r == ROUNDS - 1 else nc.gpsimd
+                adder.tensor_tensor(
                     out=result[:, 0:2].rearrange("p s i (h c) -> p (s i) h c", h=2),
                     in0=products[:, :, :, 0, :].rearrange("p s i (h c) -> p (s i) h c", h=2),
                     in1=products[:, :, :, 1, :].rearrange("p s i (h c) -> p (s i) h c", h=2)[:, :, ::-1, :],
                     op=ALU.add,
                 )
             else:
-                adder = nc.vector if r == ROUNDS - 1 else nc.gpsimd
                 for i in range(ROUND):
-                    adder.tensor_tensor(
+                    nc.gpsimd.tensor_tensor(
                         out=result[:, 0:2, i, :].rearrange("p s (h c) -> p s h c", h=2),
                         in0=products[:, :, i, 0, :].rearrange("p s (h c) -> p s h c", h=2),
                         in1=products[:, :, i, 1, :].rearrange("p s (h c) -> p s h c", h=2)[:, :, ::-1, :],

@@ -46,6 +46,18 @@ def tile_attentionhead_pa_kernel(tc, x, W_qkv_words, W_qkv_scales, sqk, out_0, o
         psum_t = ctx.enter_context(tc.psum_pool(name="psum_t", bufs=2 * ROUND))
         psum_o = ctx.enter_context(tc.psum_pool(name="psum_o", bufs=2 * ROUND))
 
+        position = consts.tile([P, TILES], F32)
+        nc.gpsimd.iota(
+            position[:], pattern=[[1, TILES]], base=0, channel_multiplier=TILES, allow_small_or_imprecise_dtypes=True
+        )
+        identity = consts.tile([P, P], F32)
+        make_identity(nc, identity[:])
+        gain_row = consts.tile([P, D], BF16)
+        nc.vector.memset(gain_row[:], 0.0)
+        nc.scalar.dma_start(out=gain_row[0:1, :], in_=sqk.unsqueeze(0))
+        ones = consts.tile([P, P], BF16)
+        nc.vector.memset(ones[:], 1.0)
+
         x_tiles = [x_pool.tile([P, C], BF16, name="x%d" % n) for n in range(B * TILES)]
 
         def load_x(n):
@@ -55,7 +67,7 @@ def tile_attentionhead_pa_kernel(tc, x, W_qkv_words, W_qkv_scales, sqk, out_0, o
             load_x(n)
 
         w_scales = consts.tile([P, PASSES, QKV * D], U8, align_bytes=64)
-        nc.vector.memset(w_scales[:].bitcast(I32), 0)
+        nc.gpsimd.memset(w_scales[:].bitcast(I32), 0)
         scale_rows = W_qkv_scales.rearrange("g (q r) n -> r q g n", r=4)
         for r in range(4):
             nc.sync.dma_start(out=w_scales[r:P:32].bitcast(I32), in_=scale_rows[r].bitcast(I32))
@@ -65,35 +77,14 @@ def tile_attentionhead_pa_kernel(tc, x, W_qkv_words, W_qkv_scales, sqk, out_0, o
         for n in range(2 * ROUND, B * TILES):
             load_x(n)
 
-        position = consts.tile([P, TILES], F32)
-        nc.gpsimd.iota(
-            position[:], pattern=[[1, TILES]], base=0, channel_multiplier=TILES, allow_small_or_imprecise_dtypes=True
-        )
-        identity = consts.tile([P, P], F32)
-        make_identity(nc, identity[:])
 
-        gain_row = consts.tile([P, D], BF16)
-        nc.vector.memset(gain_row[:], 0.0)
-        nc.scalar.dma_start(out=gain_row[0:1, :], in_=sqk.unsqueeze(0))
-        ones = consts.tile([P, P], BF16)
-        nc.vector.memset(ones[:], 1.0)
-
-        frequency = consts.tile([P, HALF], F32)
-        nc.vector.memset(frequency[:, 0:1], 1.0)
-        for step in range(int(math.log2(HALF))):
-            w = 2**step
-            nc.vector.tensor_scalar_mul(
-                out=frequency[:, w : 2 * w], in0=frequency[:, 0:w], scalar1=ROPE_BASE ** (-2.0 * w / D)
-            )
-        position_turns = consts.tile([P, TILES], F32)
-        nc.vector.tensor_scalar_mul(out=position_turns[:], in0=position[:], scalar1=1.0 / (2.0 * math.pi))
         turns = consts.tile([P, TILES, HALF], F32)
-        nc.vector.tensor_tensor(
-            out=turns[:],
-            in0=position_turns[:].unsqueeze(2).to_broadcast([P, TILES, HALF]),
-            in1=frequency[:].unsqueeze(1).to_broadcast([P, TILES, HALF]),
-            op=ALU.mult,
-        )
+        nc.vector.tensor_scalar_mul(out=turns[:, :, 0:1], in0=position[:].unsqueeze(2), scalar1=1.0 / (2.0 * math.pi))
+        for w in (1, 4, 16):
+            for m in (1, 2, 3):
+                nc.vector.tensor_scalar_mul(
+                    out=turns[:, :, m * w : (m + 1) * w], in0=turns[:, :, 0:w], scalar1=ROPE_BASE ** (-2.0 * m * w / D)
+                )
         whole = consts.tile([P, TILES, HALF], F32)
         nc.vector.tensor_scalar(
             out=whole[:], in0=turns[:], scalar1=ROUND_MAGIC, scalar2=ROUND_MAGIC, op0=ALU.add, op1=ALU.subtract
@@ -107,8 +98,6 @@ def tile_attentionhead_pa_kernel(tc, x, W_qkv_words, W_qkv_scales, sqk, out_0, o
         cos_sin = consts.tile([P, 2, TILES, HALF], F32)
         nc.scalar.activation(out=cos_sin[:, 1], in_=part_turn[:], func=ACT.Sin, scale=2.0 * math.pi)
         nc.scalar.activation(out=cos_sin[:, 0], in_=part_turn_abs[:], func=ACT.Sin, scale=-2.0 * math.pi, bias=math.pi / 2.0)
-        table_load = consts.tile([P, 1], F32)
-        nc.scalar.activation(out=table_load[:], in_=frequency[:, 0:1], func=ACT.Abs_reciprocal_sqrt)
 
         tables = consts.tile([P, TILES, 2, D], F32)
 
@@ -119,6 +108,8 @@ def tile_attentionhead_pa_kernel(tc, x, W_qkv_words, W_qkv_scales, sqk, out_0, o
             nc.scalar.copy(out=gains[:, 0, :], in_=gain[:])
             nc.scalar.copy(out=gains[:, 1, 0:HALF], in_=gain[:, HALF:D])
             nc.scalar.mul(out=gains[:, 1, HALF:D], in_=gain[:, 0:HALF], mul=-1.0)
+            table_load = consts.tile([P, 1], F32)
+            nc.scalar.activation(out=table_load[:], in_=ones[:, 0:1], func=ACT.Abs_reciprocal_sqrt)
             for part in range(ROUNDS_PER_BATCH):
                 tiles = slice(part * ROUND, (part + 1) * ROUND)
                 for i in range(2):

@@ -129,7 +129,7 @@ def tile_attentionhead_pa_kernel(tc, x, W_qkv_words, W_qkv_scales, sqk, out_0, o
             grouped_words = grouped[r][:].bitcast(F32).rearrange("p (i g t u) -> p i g t u", i=ROUND, g=PASSES, u=2)
             for i in range(ROUND):
                 x_words = x_tiles[r * ROUND + i][:].bitcast(F32)
-                xt = psum_t.tile([P, PASSES, 2, P], F32)
+                xt = psum_t.tile([P, PASSES, 2, P], F32, tag="xt")
                 for g in range(PASSES):
                     for u in range(2):
                         first = g * WORDS_PER_PASS + u
@@ -159,29 +159,46 @@ def tile_attentionhead_pa_kernel(tc, x, W_qkv_words, W_qkv_scales, sqk, out_0, o
             result = results.tile([P, QKV, ROUND, D], F32)
             sum_squares = stage.tile([P, ROUND, 2], F32)
             inverse_norm = stage.tile([P, ROUND, 2], F32)
+
+            def product(out, i, s):
+                for g in range(PASSES):
+                    nc.tensor.matmul_mx(
+                        out=out,
+                        lhsT=x_codes[:, i, g, :].bitcast(FP8X4),
+                        lhsT_scale=x_scales[:, i, g, :],
+                        rhs=w_words[:, g, 2 * D * s : 2 * D * (s + 1)].bitcast(FP4X4),
+                        rhs_scale=w_scales[:, g, D * s : D * (s + 1)],
+                        start=(g == 0),
+                        stop=(g == PASSES - 1),
+                    )
+
             banks = []
             for i in range(ROUND):
-                qkv = psum_o.tile([P, QKV, D], F32)
-                banks.append(qkv)
-                for s in range(QKV):
-                    for g in range(PASSES):
-                        nc.tensor.matmul_mx(
-                            out=qkv[:, s, :],
-                            lhsT=x_codes[:, i, g, :].bitcast(FP8X4),
-                            lhsT_scale=x_scales[:, i, g, :],
-                            rhs=w_words[:, g, 2 * D * s : 2 * D * (s + 1)].bitcast(FP4X4),
-                            rhs_scale=w_scales[:, g, D * s : D * (s + 1)],
-                            start=(g == 0),
-                            stop=(g == PASSES - 1),
-                        )
-            for i in range(ROUND):
-                squares = stage.tile([P, 2, D], BF16)
+                qk = psum_o.tile([P, 2, D], F32)
+                banks.append(qk)
                 for s in range(2):
-                    nc.scalar.activation(
-                        out=squares[:, s, :], in_=banks[i][:, s, :], func=ACT.Square, accum_out=sum_squares[:, i, s : s + 1]
-                    )
-                nc.scalar.copy(out=result[:, 2, i, :], in_=banks[i][:, 2, :])
+                    product(qk[:, s, :], i, s)
+            values = psum_t.tile([P, ROUND, D], F32, tag="xt")
+            for i in range(ROUND):
+                product(values[:, i, :], i, 2)
+
+            squares = stage.tile([P, ROUND, 2, D], BF16)
+
+            def square(i, s):
+                nc.scalar.activation(
+                    out=squares[:, i, s, :], in_=banks[i][:, s, :], func=ACT.Square, accum_out=sum_squares[:, i, s : s + 1]
+                )
+
+            def invert(i):
                 nc.scalar.activation(out=inverse_norm[:, i], in_=sum_squares[:, i], func=ACT.Abs_reciprocal_sqrt)
+
+            square(0, 0)
+            square(0, 1)
+            square(1, 0)
+            invert(0)
+            square(1, 1)
+            nc.scalar.copy(out=result[:, 2], in_=values[:])
+            invert(1)
             b, part = divmod(r, ROUNDS_PER_BATCH)
             nc.sync.dma_start(out=out_rows[2][b][:, part * ROUND : (part + 1) * ROUND, :], in_=result[:, 2])
             projected[r] = (banks, inverse_norm, result)
@@ -224,9 +241,9 @@ def tile_attentionhead_pa_kernel(tc, x, W_qkv_words, W_qkv_scales, sqk, out_0, o
                 transpose_round(step)
             if step == 0:
                 build_tables()
+            if 1 <= step <= ROUNDS:
+                project_round(step - 1)
             if step >= 2:
                 rotate_round(step - 2)
             if step < ROUNDS:
                 quantise_round(step)
-            if 1 <= step <= ROUNDS:
-                project_round(step - 1)

@@ -29,6 +29,9 @@ ROUNDS = B * ROUNDS_PER_BATCH
 QKV = 3
 ROUND_MAGIC = 1.5 * 2.0**23
 
+WARM_FIRST = 11
+WARM_NEXT = 4
+
 FLOPS = 2 * B * T * C * QKV * D
 
 
@@ -52,11 +55,19 @@ def tile_attentionhead_pa_kernel(tc, x, W_qkv_words, W_qkv_scales, sqk, out_0, o
         )
         identity = consts.tile([P, P], F32)
         make_identity(nc, identity[:])
+        ones = consts.tile([P, P], BF16)
+        nc.vector.memset(ones[:], 1.0)
         gain_row = consts.tile([P, D], BF16)
         nc.vector.memset(gain_row[:], 0.0)
         nc.scalar.dma_start(out=gain_row[0:1, :], in_=sqk.unsqueeze(0))
-        ones = consts.tile([P, P], BF16)
-        nc.vector.memset(ones[:], 1.0)
+
+        warm = psum_o.tile([P, P], F32, tag="qk")
+
+        def warm_up(matmuls):
+            for n in range(matmuls):
+                nc.tensor.matmul(out=warm[:], lhsT=ones[:], rhs=ones[:], start=True, stop=True)
+
+        warm_up(WARM_FIRST)
 
         x_tiles = [x_pool.tile([P, C], BF16, name="x%d" % n) for n in range(B * TILES)]
 
@@ -174,7 +185,7 @@ def tile_attentionhead_pa_kernel(tc, x, W_qkv_words, W_qkv_scales, sqk, out_0, o
 
             banks = []
             for i in range(ROUND):
-                qk = psum_o.tile([P, 2, D], F32)
+                qk = psum_o.tile([P, 2, D], F32, tag="qk")
                 banks.append(qk)
                 for s in range(2):
                     product(qk[:, s, :], i, s)
@@ -240,6 +251,7 @@ def tile_attentionhead_pa_kernel(tc, x, W_qkv_words, W_qkv_scales, sqk, out_0, o
             if step < ROUNDS:
                 transpose_round(step)
             if step == 0:
+                warm_up(WARM_NEXT)
                 build_tables()
             if 1 <= step <= ROUNDS:
                 project_round(step - 1)

@@ -228,24 +228,34 @@ def tile_attentionhead_pa_kernel(tc, x, W_qkv_words, W_qkv_scales, sqk, out_0, o
                         op0=ALU.mult,
                         op1=ALU.mult,
                     )
-            if r != ROUNDS - 2:
-                adder = nc.vector if r == ROUNDS - 1 else nc.gpsimd
-                adder.tensor_tensor(
-                    out=result[:, 0:2].rearrange("p s i (h c) -> p (s i) h c", h=2),
-                    in0=products[:, :, :, 0, :].rearrange("p s i (h c) -> p (s i) h c", h=2),
-                    in1=products[:, :, :, 1, :].rearrange("p s i (h c) -> p (s i) h c", h=2)[:, :, ::-1, :],
+            def add(engine, out, first, second):
+                engine.tensor_tensor(
+                    out=out.rearrange("p n (h c) -> p n h c", h=2),
+                    in0=first.rearrange("p n (h c) -> p n h c", h=2),
+                    in1=second.rearrange("p n (h c) -> p n h c", h=2)[:, :, ::-1, :],
                     op=ALU.add,
                 )
-            else:
+
+            rows = out_rows[0:2]
+            tiles = slice(part * ROUND, (part + 1) * ROUND)
+            if r < ROUNDS - 2:
+                add(
+                    nc.gpsimd,
+                    result[:, 0:2].rearrange("p s i j -> p (s i) j"),
+                    products[:, :, :, 0].rearrange("p s i j -> p (s i) j"),
+                    products[:, :, :, 1].rearrange("p s i j -> p (s i) j"),
+                )
+                for s in range(2):
+                    nc.sync.dma_start(out=rows[s][b][:, tiles, :], in_=result[:, s])
+            elif r == ROUNDS - 2:
                 for i in range(ROUND):
-                    nc.gpsimd.tensor_tensor(
-                        out=result[:, 0:2, i, :].rearrange("p s (h c) -> p s h c", h=2),
-                        in0=products[:, :, i, 0, :].rearrange("p s (h c) -> p s h c", h=2),
-                        in1=products[:, :, i, 1, :].rearrange("p s (h c) -> p s h c", h=2)[:, :, ::-1, :],
-                        op=ALU.add,
-                    )
-            for s in range(2):
-                nc.sync.dma_start(out=out_rows[s][b][:, part * ROUND : (part + 1) * ROUND, :], in_=result[:, s])
+                    add(nc.gpsimd, result[:, 0:2, i], products[:, :, i, 0], products[:, :, i, 1])
+                    for s in range(2):
+                        nc.sync.dma_start(out=rows[s][b][:, part * ROUND + i, :], in_=result[:, s, i])
+            else:
+                for s in range(2):
+                    add(nc.vector, result[:, s], products[:, s, :, 0], products[:, s, :, 1])
+                    nc.sync.dma_start(out=rows[s][b][:, tiles, :], in_=result[:, s])
 
         for step in range(ROUNDS + 2):
             if step < ROUNDS:

import math
from contextlib import ExitStack

import concourse.mybir as mybir
from concourse.masks import make_identity

F32 = mybir.dt.float32
BF16 = mybir.dt.bfloat16
I32 = mybir.dt.int32
U32 = mybir.dt.uint32
U8 = mybir.dt.uint8
FP8X4 = mybir.dt.float8_e4m3fn_x4
FP4X4 = mybir.dt.float4_e2m1fn_x4
ALU = mybir.AluOpType
ACT = mybir.ActivationFunctionType

B, T, C, D = 4, 512, 1024, 128
ROPE_BASE = 10000.0
HALF = D // 2
P = 128
PACK = 4
K_PASS = P * PACK
PASSES = C // K_PASS
WORDS_PER_PASS = K_PASS // 2
TILES = T // P
ROUND = 2
ROUNDS_PER_BATCH = TILES // ROUND
ROUNDS = B * ROUNDS_PER_BATCH
QKV = 3
ROUND_MAGIC = 1.5 * 2.0**23

WARM_FIRST = 11
WARM_NEXT = 4

FLOPS = 2 * B * T * C * QKV * D


def tile_attentionhead_pa_kernel(tc, x, W_qkv_words, W_qkv_scales, sqk, out_0, out_1, out_2):
    nc = tc.nc
    x_rows = x.rearrange("b (p a) k -> b p a k", a=TILES)
    out_rows = [o.rearrange("b (p a) j -> b p a j", a=TILES) for o in (out_0, out_1, out_2)]

    with ExitStack() as ctx:
        ctx.enter_context(tc.manual_schedule())
        consts = ctx.enter_context(tc.tile_pool(name="consts", bufs=1))
        x_pool = ctx.enter_context(tc.tile_pool(name="x_pool", bufs=1))
        stage = ctx.enter_context(tc.tile_pool(name="stage", bufs=3))
        results = ctx.enter_context(tc.tile_pool(name="results", bufs=ROUNDS))
        psum_t = ctx.enter_context(tc.psum_pool(name="psum_t", bufs=2 * ROUND))
        psum_o = ctx.enter_context(tc.psum_pool(name="psum_o", bufs=2 * ROUND))

        position = consts.tile([P, TILES], F32)
        nc.gpsimd.iota(
            position[:], pattern=[[1, TILES]], base=0, channel_multiplier=TILES, allow_small_or_imprecise_dtypes=True
        )
        identity = consts.tile([P, P], F32)
        make_identity(nc, identity[:])
        ones = consts.tile([P, P], BF16)
        nc.vector.memset(ones[:], 1.0)
        gain_row = consts.tile([P, D], BF16)
        nc.vector.memset(gain_row[:], 0.0)
        nc.scalar.dma_start(out=gain_row[0:1, :], in_=sqk.unsqueeze(0))

        warm = psum_o.tile([P, P], F32, tag="qk")

        def warm_up(matmuls):
            for n in range(matmuls):
                nc.tensor.matmul(out=warm[:], lhsT=ones[:], rhs=ones[:], start=True, stop=True)

        warm_up(WARM_FIRST)

        x_tiles = [x_pool.tile([P, C], BF16, name="x%d" % n) for n in range(B * TILES)]

        def load_x(n):
            nc.sync.dma_start(out=x_tiles[n][:], in_=x_rows[n // TILES][:, n % TILES, :])

        for n in range(2 * ROUND):
            load_x(n)

        w_scales = consts.tile([P, PASSES, QKV * D], U8, align_bytes=64)
        nc.gpsimd.memset(w_scales[:].bitcast(I32), 0)
        scale_rows = W_qkv_scales.rearrange("g (q r) n -> r q g n", r=4)
        for r in range(4):
            nc.sync.dma_start(out=w_scales[r:P:32].bitcast(I32), in_=scale_rows[r].bitcast(I32))
        w_words = consts.tile([P, PASSES, 2 * QKV * D], U8, align_bytes=64)
        nc.sync.dma_start(out=w_words[:].bitcast(I32), in_=W_qkv_words.rearrange("g p n -> p g n").bitcast(I32))

        for n in range(2 * ROUND, B * TILES):
            load_x(n)


        turns = consts.tile([P, TILES, HALF], F32)
        nc.vector.tensor_scalar_mul(out=turns[:, :, 0:1], in0=position[:].unsqueeze(2), scalar1=1.0 / (2.0 * math.pi))
        for w in (1, 4, 16):
            for m in (1, 2, 3):
                nc.vector.tensor_scalar_mul(
                    out=turns[:, :, m * w : (m + 1) * w], in0=turns[:, :, 0:w], scalar1=ROPE_BASE ** (-2.0 * m * w / D)
                )
        whole = consts.tile([P, TILES, HALF], F32)
        nc.vector.tensor_scalar(
            out=whole[:], in0=turns[:], scalar1=ROUND_MAGIC, scalar2=ROUND_MAGIC, op0=ALU.add, op1=ALU.subtract
        )
        part_turn = consts.tile([P, TILES, HALF], F32)
        nc.vector.tensor_sub(out=part_turn[:], in0=turns[:], in1=whole[:])
        part_turn_abs = consts.tile([P, TILES, HALF], F32)
        nc.vector.scalar_tensor_tensor(
            out=part_turn_abs[:], in0=part_turn[:], scalar=-1.0, in1=part_turn[:], op0=ALU.mult, op1=ALU.max
        )
        cos_sin = consts.tile([P, 2, TILES, HALF], F32)
        nc.scalar.activation(out=cos_sin[:, 1], in_=part_turn[:], func=ACT.Sin, scale=2.0 * math.pi)
        nc.scalar.activation(out=cos_sin[:, 0], in_=part_turn_abs[:], func=ACT.Sin, scale=-2.0 * math.pi, bias=math.pi / 2.0)

        tables = consts.tile([P, TILES, 2, D], F32)

        def build_tables():
            gain = psum_t.tile([P, D], F32, tag="xt")
            nc.tensor.matmul(out=gain[:], lhsT=ones[:], rhs=gain_row[:], start=True, stop=True)
            gains = consts.tile([P, 2, D], F32)
            nc.scalar.copy(out=gains[:, 0, :], in_=gain[:])
            nc.scalar.copy(out=gains[:, 1, 0:HALF], in_=gain[:, HALF:D])
            nc.scalar.mul(out=gains[:, 1, HALF:D], in_=gain[:, 0:HALF], mul=-1.0)
            table_load = consts.tile([P, 1], F32)
            nc.scalar.activation(out=table_load[:], in_=ones[:, 0:1], func=ACT.Abs_reciprocal_sqrt)
            for part in range(ROUNDS_PER_BATCH):
                tiles = slice(part * ROUND, (part + 1) * ROUND)
                for i in range(2):
                    nc.gpsimd.tensor_tensor(
                        out=tables[:, tiles, i, :].rearrange("p a (h c) -> p a h c", h=2),
                        in0=cos_sin[:, i, tiles].unsqueeze(2).to_broadcast([P, ROUND, 2, HALF]),
                        in1=gains[:, i, :].rearrange("p (h c) -> p h c", h=2).unsqueeze(1).to_broadcast([P, ROUND, 2, HALF]),
                        op=ALU.mult,
                    )

        grouped = {}
        quantised = {}
        projected = {}

        def transpose_round(r):
            grouped[r] = stage.tile([P, ROUND * PASSES * P * PACK], BF16, align_bytes=64, name="grouped")
            grouped_words = grouped[r][:].bitcast(F32).rearrange("p (i g t u) -> p i g t u", i=ROUND, g=PASSES, u=2)
            for i in range(ROUND):
                x_words = x_tiles[r * ROUND + i][:].bitcast(F32)
                xt = psum_t.tile([P, PASSES, 2, P], F32, tag="xt")
                for g in range(PASSES):
                    for u in range(2):
                        first = g * WORDS_PER_PASS + u
                        nc.tensor.transpose(xt[:, g, u, :], x_words[:, first : (g + 1) * WORDS_PER_PASS : 2], identity[:])
                if r < 2:
                    nc.vector.tensor_copy(out=grouped_words[:, i], in_=xt[:].rearrange("p g u t -> p g t u"))
                elif i == 0:
                    nc.vector.tensor_copy(out=grouped_words[:, i, 0], in_=xt[:, 0].rearrange("p u t -> p t u"))
                    nc.scalar.copy(out=grouped_words[:, i, 1], in_=xt[:, 1].rearrange("p u t -> p t u"))
                else:
                    nc.scalar.copy(out=grouped_words[:, i], in_=xt[:].rearrange("p g u t -> p g t u"))

        def quantise_round(r):
            x_codes = stage.tile([P, ROUND, PASSES, P], U32, align_bytes=64)
            x_scales = stage.tile([P, ROUND, PASSES, P], U8, align_bytes=64)
            tile_values = PASSES * P * PACK
            for i in range(ROUND):
                nc.vector.quantize_mx(
                    out=x_codes[:, i].rearrange("p g t -> p (g t)").bitcast(FP8X4),
                    scales=x_scales[:, i].rearrange("p g t -> p (g t)"),
                    in_=grouped[r][:, i * tile_values : (i + 1) * tile_values],
                )
            quantised[r] = (x_codes, x_scales)

        def project_round(r):
            x_codes, x_scales = quantised[r]
            result = results.tile([P, QKV, ROUND, D], F32)
            sum_squares = stage.tile([P, ROUND, 2], F32)
            inverse_norm = stage.tile([P, ROUND, 2], F32)

            def product(out, i, s):
                for g in range(PASSES):
                    nc.tensor.matmul_mx(
                        out=out,
                        lhsT=x_codes[:, i, g, :].bitcast(FP8X4),
                        lhsT_scale=x_scales[:, i, g, :],
                        rhs=w_words[:, g, 2 * D * s : 2 * D * (s + 1)].bitcast(FP4X4),
                        rhs_scale=w_scales[:, g, D * s : D * (s + 1)],
                        start=(g == 0),
                        stop=(g == PASSES - 1),
                    )

            banks = []
            for i in range(ROUND):
                qk = psum_o.tile([P, 2, D], F32, tag="qk")
                banks.append(qk)
                for s in range(2):
                    product(qk[:, s, :], i, s)
            values = psum_t.tile([P, ROUND, D], F32, tag="xt")
            for i in range(ROUND):
                product(values[:, i, :], i, 2)

            squares = stage.tile([P, ROUND, 2, D], BF16)

            def square(i, s):
                nc.scalar.activation(
                    out=squares[:, i, s, :], in_=banks[i][:, s, :], func=ACT.Square, accum_out=sum_squares[:, i, s : s + 1]
                )

            def invert(i):
                nc.scalar.activation(out=inverse_norm[:, i], in_=sum_squares[:, i], func=ACT.Abs_reciprocal_sqrt)

            square(0, 0)
            square(0, 1)
            square(1, 0)
            invert(0)
            square(1, 1)
            nc.scalar.copy(out=result[:, 2], in_=values[:])
            invert(1)
            b, part = divmod(r, ROUNDS_PER_BATCH)
            nc.sync.dma_start(out=out_rows[2][b][:, part * ROUND : (part + 1) * ROUND, :], in_=result[:, 2])
            projected[r] = (banks, inverse_norm, result)

        def rotate_round(r):
            banks, inverse_norm, result = projected[r]
            b, part = divmod(r, ROUNDS_PER_BATCH)
            products = stage.tile([P, 2, ROUND, 2, D], F32)
            for i in range(ROUND):
                for s in range(2):
                    nc.vector.scalar_tensor_tensor(
                        out=products[:, s, i],
                        in0=banks[i][:, s, :].unsqueeze(1).to_broadcast([P, 2, D]),
                        scalar=inverse_norm[:, i, s : s + 1],
                        in1=tables[:, part * ROUND + i],
                        op0=ALU.mult,
                        op1=ALU.mult,
                    )
            def add(engine, out, first, second):
                engine.tensor_tensor(
                    out=out.rearrange("p n (h c) -> p n h c", h=2),
                    in0=first.rearrange("p n (h c) -> p n h c", h=2),
                    in1=second.rearrange("p n (h c) -> p n h c", h=2)[:, :, ::-1, :],
                    op=ALU.add,
                )

            rows = out_rows[0:2]
            tiles = slice(part * ROUND, (part + 1) * ROUND)
            if r < ROUNDS - 2:
                add(
                    nc.gpsimd,
                    result[:, 0:2].rearrange("p s i j -> p (s i) j"),
                    products[:, :, :, 0].rearrange("p s i j -> p (s i) j"),
                    products[:, :, :, 1].rearrange("p s i j -> p (s i) j"),
                )
                for s in range(2):
                    nc.sync.dma_start(out=rows[s][b][:, tiles, :], in_=result[:, s])
            elif r == ROUNDS - 2:
                for i in range(ROUND):
                    add(nc.gpsimd, result[:, 0:2, i], products[:, :, i, 0], products[:, :, i, 1])
                    for s in range(2):
                        nc.sync.dma_start(out=rows[s][b][:, part * ROUND + i, :], in_=result[:, s, i])
            else:
                for s in range(2):
                    add(nc.vector, result[:, s], products[:, s, :, 0], products[:, s, :, 1])
                    nc.sync.dma_start(out=rows[s][b][:, tiles, :], in_=result[:, s])

        for step in range(ROUNDS + 2):
            if step < ROUNDS:
                transpose_round(step)
            if step == 0:
                warm_up(WARM_NEXT)
                build_tables()
            if 1 <= step <= ROUNDS:
                project_round(step - 1)
            if step >= 2:
                rotate_round(step - 2)
            if step < ROUNDS:
                quantise_round(step)
